import numpy as np
import ml_dtypes


def mxq(x, axis, fmt="e4m3"):
    dtype, down = {"e4m3": (ml_dtypes.float8_e4m3fn, 7), "e5m2": (ml_dtypes.float8_e5m2, 14)}[fmt]
    v = np.moveaxis(np.asarray(x, np.float32).astype(ml_dtypes.bfloat16).astype(np.float64), axis, -1)
    blocks = v.reshape(v.shape[:-1] + (-1, 32))
    amax = np.abs(blocks).max(-1, keepdims=True)
    byte = np.maximum(np.where(amax > 0, np.frexp(amax)[1] - 1 + 127, 0) - down, 1)
    scale = np.exp2(byte - 127.0)
    codes = (blocks / scale).astype(np.float32).astype(dtype).astype(np.float64)
    return np.moveaxis((codes * scale).reshape(v.shape), -1, axis)


WIDE = False


def mx_kscale(k):
    if not WIDE:
        return np.ones(k)
    levels = np.array([10, -10, 5, -5, 0])
    a = np.random.permutation(np.resize(levels, k // 512 * 4)).reshape(k // 512, 4)
    idx = np.arange(k)
    return np.exp2(a[idx // 512, idx % 128 // 32])


BF16 = ml_dtypes.bfloat16


def bf(x):
    return np.asarray(x, np.float32).astype(BF16)


def f64(x):
    return np.asarray(x).astype(np.float64)


B, SIDE, HE, Z, HD, XO = 4096, 32, 1024, 512, 256, 1024


def setup_inputs():
    n = np.random.standard_normal
    s, t = mx_kscale(HE), mx_kscale(Z)
    return {"h": bf(np.tanh(n((B, HE))) * s),
            "W_mu_e": bf(n((Z, HE)) * 1.5 / np.sqrt(HE) / s[None, :] * t[:, None]),
            "b_mu_e": bf(n(Z) * 0.3 * t),
            "W_ls_e": bf(n((Z, HE)) * 1.5 / np.sqrt(HE) / s[None, :]),
            "b_ls_e": bf(n(Z) * 0.3),
            "eps_z": bf(n((B, Z)) * t),
            "W_in_d": bf(n((HD, Z)) * 0.6 / np.sqrt(Z) / t[None, :]),
            "b_in_d": bf(n(HD) * 0.3)}


def reference(h, W_mu_e, b_mu_e, W_ls_e, b_ls_e, eps_z, W_in_d, b_in_d):
    hq = mxq(f64(h), 1, "e4m3")
    mu_e = (hq @ mxq(f64(W_mu_e), 1, "e4m3").T) + f64(b_mu_e)
    ls_e = (hq @ mxq(f64(W_ls_e), 1, "e4m3").T) + f64(b_ls_e)
    z = mu_e + np.exp(0.5 * ls_e) * f64(eps_z)
    return np.tanh((mxq(z, 1, "e4m3") @ mxq(f64(W_in_d), 1, "e4m3").T) + f64(b_in_d))

@@ -1,0 +1,388 @@
+from contextlib import ExitStack
+
+import concourse.mybir as mybir
+from concourse.masks import make_identity
+
+F32 = mybir.dt.float32
+BF16 = mybir.dt.bfloat16
+U32 = mybir.dt.uint32
+U8 = mybir.dt.uint8
+FP8X4 = mybir.dt.float8_e4m3fn_x4
+AF = mybir.ActivationFunctionType
+ALU = mybir.AluOpType
+
+P = 128
+B, HE, Z, HD = 4096, 1024, 512, 256
+FLOPS = 2 * B * HE * 2 * Z + 2 * B * Z * HD
+
+CHUNK_TILES = [4, 4, 4, 4, 4, 4, 4, 4]
+MANUAL = True
+REGROUP = "pool"
+
+
+def tile_vae_pa_t_kernel(
+    tc, h, W_mu_e, b_mu_e, W_ls_e, b_ls_e, eps_z, W_in_d, b_in_d, out
+):
+    nc = tc.nc
+    n_chunks = len(CHUNK_TILES)
+    row0 = [P * sum(CHUNK_TILES[:c]) for c in range(n_chunks)]
+    width = [P * nb for nb in CHUNK_TILES]
+
+    with ExitStack() as ctx:
+        const = ctx.enter_context(tc.tile_pool(name="const", bufs=1))
+        loads = ctx.enter_context(tc.tile_pool(name="loads", bufs=n_chunks))
+        gpool = ctx.enter_context(tc.tile_pool(name="gpool", bufs=4))
+        wpool = ctx.enter_context(tc.tile_pool(name="wpool", bufs=6))
+        spool = ctx.enter_context(tc.tile_pool(name="spool", bufs=4))
+        zpool = ctx.enter_context(tc.tile_pool(name="zpool", bufs=2))
+        zwpool = ctx.enter_context(tc.tile_pool(name="zwpool", bufs=3))
+        opool = ctx.enter_context(tc.tile_pool(name="opool", bufs=8))
+        ps_xy = ctx.enter_context(tc.psum_pool(name="ps_xy", bufs=2))
+        ps_e = ctx.enter_context(tc.psum_pool(name="ps_e", bufs=1))
+        ps_o = ctx.enter_context(tc.psum_pool(name="ps_o", bufs=1))
+        ps_mm = ctx.enter_context(tc.psum_pool(name="ps_mm", bufs=4))
+        if MANUAL:
+            ctx.enter_context(tc.manual_schedule())
+
+        w_raw = {}
+        for u in range(2):
+            for which, src in (("ls", W_ls_e), ("mu", W_mu_e)):
+                w_raw[(which, u)] = const.tile(
+                    [P, 2 * HE], BF16, name="wraw_%s%d" % (which, u), tag="wraw_%s%d" % (which, u)
+                )
+        win_raw = const.tile([P, 2 * Z], BF16, name="win_raw", tag="win_raw")
+        h_sb = [loads.tile([P, 4 * HE], BF16, name="h_sb", tag="h_sb") for c in range(n_chunks)]
+        e_sb = [loads.tile([P, 4 * Z], BF16, name="e_sb", tag="e_sb") for c in range(n_chunks)]
+
+        def load_w(which, src, u):
+            nc.sync.dma_start(
+                out=w_raw[(which, u)][:],
+                in_=src[256 * u : 256 * (u + 1), :].rearrange("(p e) k -> p (e k)", e=2),
+            )
+
+        def load_h(c):
+            nb = CHUNK_TILES[c]
+            nc.sync.dma_start(
+                out=h_sb[c][:, : nb * HE],
+                in_=h[row0[c] : row0[c] + width[c], :].rearrange("(p i) k -> p (i k)", i=nb),
+            )
+
+        def load_e(c):
+            nb = CHUNK_TILES[c]
+            nc.sync.dma_start(
+                out=e_sb[c][:, : nb * Z],
+                in_=eps_z[row0[c] : row0[c] + width[c], :].rearrange("(p i) k -> p (i k)", i=nb),
+            )
+
+        bmu_raw = const.tile([P, 4], BF16, name="bmu_raw", tag="bmu_raw")
+        bls_raw = const.tile([P, 4], BF16, name="bls_raw", tag="bls_raw")
+        bin_row = const.tile([P, HD], BF16, name="bin_row", tag="bin_row")
+        ones = const.tile([P, P], BF16, name="ones", tag="ones")
+        warm = const.tile([P, 1], F32, name="warm", tag="warm")
+        warm2 = const.tile([P, 1], F32, name="warm2", tag="warm2")
+        nc.vector.memset(warm[:], 0.0)
+        nc.vector.memset(bin_row[:], 0.0)
+        nc.vector.memset(ones[:], 1.0)
+        nc.scalar.dma_start(
+            out=bls_raw[:].rearrange("p (u e) -> p u e", u=2),
+            in_=b_ls_e.rearrange("(u p e) -> p u e", u=2, e=2),
+        )
+        nc.scalar.dma_start(
+            out=bmu_raw[:].rearrange("p (u e) -> p u e", u=2),
+            in_=b_mu_e.rearrange("(u p e) -> p u e", u=2, e=2),
+        )
+        nc.scalar.dma_start(out=bin_row[0:1, :], in_=b_in_d.rearrange("(o n) -> o n", o=1))
+        nc.scalar.activation(out=warm2[:], in_=warm[:], func=AF.Exp)
+
+        load_w("ls", W_ls_e, 0)
+        load_w("mu", W_mu_e, 0)
+        load_h(0)
+        load_w("ls", W_ls_e, 1)
+        load_w("mu", W_mu_e, 1)
+        load_e(0)
+        nc.sync.dma_start(
+            out=win_raw[:].rearrange("p (j k) -> p j k", j=2),
+            in_=W_in_d.rearrange("(j p) k -> p j k", j=2),
+        )
+        for c in range(1, n_chunks):
+            load_h(c)
+            load_e(c)
+
+        ident = const.tile([P, P], F32, name="ident", tag="ident")
+        make_identity(nc, ident[:])
+
+        bmu = const.tile([P, 4], F32, name="bmu", tag="bmu")
+        blsh = const.tile([P, 4], F32, name="blsh", tag="blsh")
+        nc.vector.tensor_copy(out=bmu[:], in_=bmu_raw[:])
+        nc.vector.tensor_scalar_mul(out=blsh[:], in0=bls_raw[:], scalar1=0.5)
+
+        def transpose_pairs(bank, src32, groups, stride, off):
+            view = bank[:].rearrange("p (v n) -> p v n", v=2)
+            for j, i in enumerate(groups):
+                for v in range(2):
+                    w0 = i * stride + off + v * P
+                    nc.tensor.transpose(
+                        out=view[:, v, j * P : (j + 1) * P],
+                        in_=src32[:, w0 : w0 + P],
+                        identity=ident[:],
+                    )
+
+        def copy_out(engine, bank, dst32):
+            src = bank[:].rearrange("p (v n) -> p n v", v=2)
+            dst = dst32.rearrange("p (n v) -> p n v", v=2)
+            if engine == "act":
+                nc.scalar.copy(out=dst, in_=src)
+            else:
+                nc.vector.tensor_copy(out=dst, in_=src)
+
+        def quantise(grp, cols, words, scales):
+            nc.vector.quantize_mx(
+                out=words[:, :cols].bitcast(FP8X4), scales=scales[:, :cols], in_=grp[:, : 4 * cols]
+            )
+
+        h32 = [t[:].bitcast(F32) for t in h_sb]
+        e32 = [t[:].bitcast(F32) for t in e_sb]
+        hw = {}
+        hs = {}
+
+        def new_grp():
+            return gpool.tile([P, 2048], BF16, name="grp", tag="grp", align_bytes=64)
+
+        def q_h(c, g, grp):
+            hw[(c, g)] = wpool.tile([P, 512], U32, name="hw", tag="hw", align_bytes=64)
+            hs[(c, g)] = wpool.tile([P, 512], U8, name="hs", tag="hs", align_bytes=64)
+            quantise(grp, width[c], hw[(c, g)], hs[(c, g)])
+
+        pro_count = [0]
+
+        def pro_bank():
+            k = pro_count[0]
+            pro_count[0] = k + 1
+            if k % 3 == 2:
+                return ps_xy.tile([P, 512], F32, name="xy", tag="xy")
+            return ps_mm.tile([P, 512], F32, name="acc", tag="acc")
+
+        ww = {}
+        ws = {}
+        pending = []
+        done_count = [0]
+
+        def flush():
+            for fn in pending[done_count[0] :]:
+                fn()
+            done_count[0] = len(pending)
+
+        def prep_w(which, u):
+            raw32 = w_raw[(which, u)][:].bitcast(F32)
+            grp = new_grp()
+            g32 = grp[:].bitcast(F32)
+            banks = []
+            for g in range(2):
+                bank = pro_bank()
+                transpose_pairs(bank, raw32, [0, 1], 512, g * 256)
+                banks.append(bank)
+            copy_out("act", banks[0], g32[:, 0:512])
+            copy_out("dve", banks[1], g32[:, 512:1024])
+            flush()
+            name = "%s%d" % (which, u)
+            ww[(which, u)] = const.tile([P, 512], U32, name="ww" + name, tag="ww" + name, align_bytes=64)
+            ws[(which, u)] = const.tile([P, 512], U8, name="ws" + name, tag="ws" + name, align_bytes=64)
+            pending.append(lambda: quantise(grp, 512, ww[(which, u)], ws[(which, u)]))
+
+        def prep_h0(g):
+            grp = new_grp()
+            g32 = grp[:].bitcast(F32)
+            banks = []
+            for b2 in range(CHUNK_TILES[0] // 2):
+                bank = pro_bank()
+                transpose_pairs(bank, h32[0], [2 * b2, 2 * b2 + 1], 512, g * 256)
+                banks.append(bank)
+            for b2, bank in enumerate(banks):
+                copy_out("act" if b2 % 2 == 0 else "dve", bank, g32[:, b2 * 512 : (b2 + 1) * 512])
+            flush()
+            pending.append(lambda: q_h(0, g, grp))
+
+        prep_w("ls", 0)
+        prep_w("mu", 0)
+        prep_h0(0)
+        prep_h0(1)
+        prep_w("ls", 1)
+        prep_w("mu", 1)
+
+        win_grp = new_grp()
+        win_bank = pro_bank()
+        transpose_pairs(win_bank, win_raw[:].bitcast(F32), [0, 1], 256, 0)
+        copy_out("act", win_bank, win_grp[:].bitcast(F32)[:, 0:512])
+        flush()
+        winw = const.tile([P, HD], U32, name="winw", tag="winw", align_bytes=64)
+        wins = const.tile([P, HD], U8, name="wins", tag="wins", align_bytes=64)
+        quantise(win_grp, HD, winw, wins)
+
+        bin_bank = pro_bank()
+        nc.tensor.matmul(out=bin_bank[:, :HD], lhsT=ones[:], rhs=bin_row[:], start=True, stop=True)
+        bin_bc = const.tile([P, 2 * HD], F32, name="bin_bc", tag="bin_bc")
+        nc.vector.tensor_copy(out=bin_bc[:, :HD], in_=bin_bank[:, :HD])
+        nc.vector.tensor_copy(out=bin_bc[:, HD:], in_=bin_bank[:, :HD])
+
+        zp = {}
+        zw = {}
+        zs = {}
+
+        def mx1(which, c, u, e):
+            n = width[c]
+            acc = ps_mm.tile([P, 512], F32, name="acc", tag="acc")
+            for g in range(2):
+                col = g * 256 + e * P
+                nc.tensor.matmul_mx(
+                    out=acc[:, :n],
+                    lhsT=ww[(which, u)][:, col : col + P].bitcast(FP8X4),
+                    lhsT_scale=ws[(which, u)][:, col : col + P],
+                    rhs=hw[(c, g)][:, :n].bitcast(FP8X4),
+                    rhs_scale=hs[(c, g)][:, :n],
+                    start=(g == 0),
+                    stop=(g == 1),
+                )
+            return acc
+
+        def do_b(c, u, mu, tt):
+            n = width[c]
+            if u == 0:
+                zp[c] = zpool.tile([P, 4, 512], BF16, name="zp", tag="zp")
+            for e in range(2):
+                t = 2 * u + e
+                nc.vector.scalar_tensor_tensor(
+                    out=zp[c][:, t, :n],
+                    in0=mu[e][:, :n],
+                    scalar=bmu[:, t : t + 1],
+                    in1=tt[e][:, :n],
+                    op0=ALU.add,
+                    op1=ALU.add,
+                )
+
+        zg = {}
+
+        def regroup(c, engine):
+            n = width[c]
+            zg[c] = zpool.tile([P, 2048], BF16, name="zg", tag="zg", align_bytes=64)
+            if engine == "pool":
+                nc.gpsimd.tensor_scalar(
+                    out=zg[c][:, : 4 * n].rearrange("p (n t) -> p n t", t=4),
+                    in0=zp[c][:, :, :n].rearrange("p t n -> p n t"),
+                    scalar1=1.0,
+                    scalar2=0.0,
+                    op0=ALU.mult,
+                    op1=ALU.add,
+                )
+            else:
+                nc.vector.tensor_copy(
+                    out=zg[c][:, : 4 * n].rearrange("p (c i t) -> p c t i", i=4, t=4),
+                    in_=zp[c][:, :, :n].rearrange("p t (c i) -> p c t i", i=4),
+                )
+
+        def q_z(c):
+            zw[c] = zwpool.tile([P, 512], U32, name="zw", tag="zw", align_bytes=64)
+            zs[c] = zwpool.tile([P, 512], U8, name="zs", tag="zs", align_bytes=64)
+            quantise(zg[c], width[c], zw[c], zs[c])
+
+        def do_s(c, unit, pool, name):
+            o = pool.tile([P, 512], F32, name=name, tag=name)
+            for j in range(2):
+                i = 2 * unit + j
+                nc.tensor.matmul_mx(
+                    out=o[:, j * HD : (j + 1) * HD],
+                    lhsT=zw[c][:, i * P : (i + 1) * P].bitcast(FP8X4),
+                    lhsT_scale=zs[c][:, i * P : (i + 1) * P],
+                    rhs=winw[:].bitcast(FP8X4),
+                    rhs_scale=wins[:],
+                    start=True,
+                    stop=True,
+                )
+            return (c, unit, o)
+
+        def do_add(item):
+            c, unit, o = item
+            o_sb = opool.tile([P, 512], F32, name="o_sb", tag="o_sb")
+            nc.vector.tensor_tensor(out=o_sb[:], in0=o[:], in1=bin_bc[:], op=ALU.add)
+            return (c, unit, o_sb)
+
+        def do_tanh_store(item):
+            c, unit, o_sb = item
+            nc.scalar.activation(out=o_sb[:], in_=o_sb[:], func=AF.Tanh)
+            view = out[row0[c] : row0[c] + width[c], :].rearrange(
+                "(p i) d -> p (i d)", i=CHUNK_TILES[c]
+            )
+            nc.sync.dma_start(out=view[:, unit * 512 : (unit + 1) * 512], in_=o_sb[:])
+
+        pend_b = None
+        pend_add = []
+        s_fifo = []
+        s_head = 0
+        for c in range(n_chunks):
+            n = width[c]
+            nb = CHUNK_TILES[c]
+            for u in range(2):
+                nxt = c + 1 < n_chunks
+                banks = []
+                if nxt:
+                    for b2 in range(CHUNK_TILES[c + 1] // 2):
+                        bank = ps_xy.tile([P, 512], F32, name="xy", tag="xy")
+                        transpose_pairs(bank, h32[c + 1], [2 * b2, 2 * b2 + 1], 512, u * 256)
+                        banks.append(bank)
+                e_bank = ps_e.tile([P, 512], F32, name="e_bank", tag="e_bank")
+                for i in range(nb):
+                    w0 = i * 256 + u * P
+                    nc.tensor.transpose(
+                        out=e_bank[:, i * P : (i + 1) * P], in_=e32[c][:, w0 : w0 + P], identity=ident[:]
+                    )
+                if pend_b is not None:
+                    do_b(*pend_b)
+                grp = None
+                if nxt:
+                    grp = new_grp()
+                    g32 = grp[:].bitcast(F32)
+                    for b2, bank in enumerate(banks):
+                        copy_out("act", bank, g32[:, b2 * 512 : (b2 + 1) * 512])
+                if u == 0 and c >= 1:
+                    regroup(c - 1, REGROUP)
+                added = [do_add(item) for item in pend_add]
+                pend_add = []
+                if u == 1 and c >= 1:
+                    q_z(c - 1)
+                    s_fifo.extend([(c - 1, unit) for unit in range(CHUNK_TILES[c - 1] // 2)])
+                if nxt:
+                    q_h(c + 1, u, grp)
+                ls = [mx1("ls", c, u, e) for e in range(2)]
+                if s_head < len(s_fifo):
+                    sc, su = s_fifo[s_head]
+                    s_head += 1
+                    pend_add.append(do_s(sc, su, ps_o, "o_bank"))
+                mu = [mx1("mu", c, u, e) for e in range(2)]
+                s_t = []
+                for e in range(2):
+                    t = 2 * u + e
+                    s = spool.tile([P, 512], F32, name="s", tag="s")
+                    nc.scalar.activation(
+                        out=s[:, :n], in_=ls[e][:, :n], func=AF.Exp, bias=blsh[:, t : t + 1], scale=0.5
+                    )
+                    s_t.append(s)
+                for item in added:
+                    do_tanh_store(item)
+                e_view = e_bank[:, :n].bitcast(BF16).rearrange("p (n e) -> p e n", e=2)
+                tts = []
+                for e in range(2):
+                    tt = spool.tile([P, 512], F32, name="tt", tag="tt")
+                    nc.vector.tensor_tensor(out=tt[:, :n], in0=e_view[:, e, :], in1=s_t[e][:, :n], op=ALU.mult)
+                    tts.append(tt)
+                pend_b = (c, u, mu, tts)
+
+        last = n_chunks - 1
+        do_b(*pend_b)
+        for sc, su in s_fifo[s_head:]:
+            pend_add.append(do_s(sc, su, ps_mm, "acc"))
+        regroup(last, "dve")
+        added = [do_add(item) for item in pend_add]
+        for item in added:
+            do_tanh_store(item)
+        q_z(last)
+        for unit in range(CHUNK_TILES[last] // 2):
+            do_tanh_store(do_add(do_s(last, unit, ps_mm, "acc")))

@@ -15,9 +15,10 @@ P = 128
 B, HE, Z, HD = 4096, 1024, 512, 256
 FLOPS = 2 * B * HE * 2 * Z + 2 * B * Z * HD
 
-CHUNK_TILES = [4, 4, 4, 4, 4, 4, 4, 4]
+CHUNK_TILES = [4, 4, 4, 4, 4, 4, 4, 2, 2]
 MANUAL = True
 REGROUP = "pool"
+POOL_ADD_EVERY = 0
 
 
 def tile_vae_pa_t_kernel(
@@ -30,7 +31,6 @@ def tile_vae_pa_t_kernel(
 
     with ExitStack() as ctx:
         const = ctx.enter_context(tc.tile_pool(name="const", bufs=1))
-        loads = ctx.enter_context(tc.tile_pool(name="loads", bufs=n_chunks))
         gpool = ctx.enter_context(tc.tile_pool(name="gpool", bufs=4))
         wpool = ctx.enter_context(tc.tile_pool(name="wpool", bufs=6))
         spool = ctx.enter_context(tc.tile_pool(name="spool", bufs=4))
@@ -44,34 +44,42 @@ def tile_vae_pa_t_kernel(
         if MANUAL:
             ctx.enter_context(tc.manual_schedule())
 
+        w_src = {"ls": W_ls_e, "mu": W_mu_e}
         w_raw = {}
         for u in range(2):
-            for which, src in (("ls", W_ls_e), ("mu", W_mu_e)):
-                w_raw[(which, u)] = const.tile(
-                    [P, 2 * HE], BF16, name="wraw_%s%d" % (which, u), tag="wraw_%s%d" % (which, u)
-                )
+            for which in ("ls", "mu"):
+                nm = "wraw_%s%d" % (which, u)
+                w_raw[(which, u)] = const.tile([P, 2 * HE], BF16, name=nm, tag=nm)
         win_raw = const.tile([P, 2 * Z], BF16, name="win_raw", tag="win_raw")
-        h_sb = [loads.tile([P, 4 * HE], BF16, name="h_sb", tag="h_sb") for c in range(n_chunks)]
-        e_sb = [loads.tile([P, 4 * Z], BF16, name="e_sb", tag="e_sb") for c in range(n_chunks)]
+        h_sb = [
+            const.tile([P, CHUNK_TILES[c] * HE], BF16, name="h_sb%d" % c, tag="h_sb%d" % c)
+            for c in range(n_chunks)
+        ]
+        e_sb = [
+            const.tile([P, CHUNK_TILES[c] * Z], BF16, name="e_sb%d" % c, tag="e_sb%d" % c)
+            for c in range(n_chunks)
+        ]
 
-        def load_w(which, src, u):
+        def load_w(which, u):
             nc.sync.dma_start(
                 out=w_raw[(which, u)][:],
-                in_=src[256 * u : 256 * (u + 1), :].rearrange("(p e) k -> p (e k)", e=2),
+                in_=w_src[which][256 * u : 256 * (u + 1), :].rearrange("(p e) k -> p (e k)", e=2),
             )
 
         def load_h(c):
-            nb = CHUNK_TILES[c]
             nc.sync.dma_start(
-                out=h_sb[c][:, : nb * HE],
-                in_=h[row0[c] : row0[c] + width[c], :].rearrange("(p i) k -> p (i k)", i=nb),
+                out=h_sb[c][:],
+                in_=h[row0[c] : row0[c] + width[c], :].rearrange(
+                    "(p i) k -> p (i k)", i=CHUNK_TILES[c]
+                ),
             )
 
         def load_e(c):
-            nb = CHUNK_TILES[c]
             nc.sync.dma_start(
-                out=e_sb[c][:, : nb * Z],
-                in_=eps_z[row0[c] : row0[c] + width[c], :].rearrange("(p i) k -> p (i k)", i=nb),
+                out=e_sb[c][:],
+                in_=eps_z[row0[c] : row0[c] + width[c], :].rearrange(
+                    "(p i) k -> p (i k)", i=CHUNK_TILES[c]
+                ),
             )
 
         bmu_raw = const.tile([P, 4], BF16, name="bmu_raw", tag="bmu_raw")
@@ -83,6 +91,7 @@ def tile_vae_pa_t_kernel(
         nc.vector.memset(warm[:], 0.0)
         nc.vector.memset(bin_row[:], 0.0)
         nc.vector.memset(ones[:], 1.0)
+        nc.scalar.dma_start(out=bin_row[0:1, :], in_=b_in_d.rearrange("(o n) -> o n", o=1))
         nc.scalar.dma_start(
             out=bls_raw[:].rearrange("p (u e) -> p u e", u=2),
             in_=b_ls_e.rearrange("(u p e) -> p u e", u=2, e=2),
@@ -91,30 +100,26 @@ def tile_vae_pa_t_kernel(
             out=bmu_raw[:].rearrange("p (u e) -> p u e", u=2),
             in_=b_mu_e.rearrange("(u p e) -> p u e", u=2, e=2),
         )
-        nc.scalar.dma_start(out=bin_row[0:1, :], in_=b_in_d.rearrange("(o n) -> o n", o=1))
         nc.scalar.activation(out=warm2[:], in_=warm[:], func=AF.Exp)
 
-        load_w("ls", W_ls_e, 0)
-        load_w("mu", W_mu_e, 0)
+        load_w("ls", 0)
         load_h(0)
-        load_w("ls", W_ls_e, 1)
-        load_w("mu", W_mu_e, 1)
+        load_w("mu", 0)
+        load_w("ls", 1)
+        load_w("mu", 1)
         load_e(0)
+        load_h(1)
+        load_e(1)
         nc.sync.dma_start(
             out=win_raw[:].rearrange("p (j k) -> p j k", j=2),
             in_=W_in_d.rearrange("(j p) k -> p j k", j=2),
         )
-        for c in range(1, n_chunks):
+        for c in range(2, n_chunks):
             load_h(c)
             load_e(c)
 
         ident = const.tile([P, P], F32, name="ident", tag="ident")
         make_identity(nc, ident[:])
-
-        bmu = const.tile([P, 4], F32, name="bmu", tag="bmu")
-        blsh = const.tile([P, 4], F32, name="blsh", tag="blsh")
-        nc.vector.tensor_copy(out=bmu[:], in_=bmu_raw[:])
-        nc.vector.tensor_scalar_mul(out=blsh[:], in0=bls_raw[:], scalar1=0.5)
 
         def transpose_pairs(bank, src32, groups, stride, off):
             view = bank[:].rearrange("p (v n) -> p v n", v=2)
@@ -140,97 +145,70 @@ def tile_vae_pa_t_kernel(
                 out=words[:, :cols].bitcast(FP8X4), scales=scales[:, :cols], in_=grp[:, : 4 * cols]
             )
 
+        def bank_of(pool):
+            if pool == "xy":
+                return ps_xy.tile([P, 512], F32, name="xy", tag="xy")
+            if pool == "o":
+                return ps_o.tile([P, 512], F32, name="o_bank", tag="o_bank")
+            return ps_mm.tile([P, 512], F32, name="acc", tag="acc")
+
+        def new_grp():
+            return gpool.tile([P, 2048], BF16, name="grp", tag="grp", align_bytes=64)
+
         h32 = [t[:].bitcast(F32) for t in h_sb]
         e32 = [t[:].bitcast(F32) for t in e_sb]
         hw = {}
         hs = {}
+        ww = {}
+        ws = {}
 
-        def new_grp():
-            return gpool.tile([P, 2048], BF16, name="grp", tag="grp", align_bytes=64)
+        def tr_w(which, u, pool):
+            raw32 = w_raw[(which, u)][:].bitcast(F32)
+            banks = []
+            for g in range(2):
+                bank = bank_of(pool)
+                transpose_pairs(bank, raw32, [0, 1], 512, g * 256)
+                banks.append(bank)
+            return banks
+
+        def tr_h(c, g, pool):
+            banks = []
+            for b2 in range(CHUNK_TILES[c] // 2):
+                bank = bank_of(pool)
+                transpose_pairs(bank, h32[c], [2 * b2, 2 * b2 + 1], 512, g * 256)
+                banks.append(bank)
+            return banks
+
+        def copy_banks(banks, engines):
+            grp = new_grp()
+            g32 = grp[:].bitcast(F32)
+            for k, bank in enumerate(banks):
+                copy_out(engines[k % len(engines)], bank, g32[:, k * 512 : (k + 1) * 512])
+            return grp
+
+        def q_w(which, u, grp):
+            nm = "%s%d" % (which, u)
+            ww[(which, u)] = const.tile([P, 512], U32, name="ww" + nm, tag="ww" + nm, align_bytes=64)
+            ws[(which, u)] = const.tile([P, 512], U8, name="ws" + nm, tag="ws" + nm, align_bytes=64)
+            quantise(grp, 512, ww[(which, u)], ws[(which, u)])
 
         def q_h(c, g, grp):
             hw[(c, g)] = wpool.tile([P, 512], U32, name="hw", tag="hw", align_bytes=64)
             hs[(c, g)] = wpool.tile([P, 512], U8, name="hs", tag="hs", align_bytes=64)
             quantise(grp, width[c], hw[(c, g)], hs[(c, g)])
 
-        pro_count = [0]
-
-        def pro_bank():
-            k = pro_count[0]
-            pro_count[0] = k + 1
-            if k % 3 == 2:
-                return ps_xy.tile([P, 512], F32, name="xy", tag="xy")
-            return ps_mm.tile([P, 512], F32, name="acc", tag="acc")
-
-        ww = {}
-        ws = {}
-        pending = []
-        done_count = [0]
-
-        def flush():
-            for fn in pending[done_count[0] :]:
-                fn()
-            done_count[0] = len(pending)
-
-        def prep_w(which, u):
-            raw32 = w_raw[(which, u)][:].bitcast(F32)
-            grp = new_grp()
-            g32 = grp[:].bitcast(F32)
-            banks = []
-            for g in range(2):
-                bank = pro_bank()
-                transpose_pairs(bank, raw32, [0, 1], 512, g * 256)
-                banks.append(bank)
-            copy_out("act", banks[0], g32[:, 0:512])
-            copy_out("dve", banks[1], g32[:, 512:1024])
-            flush()
-            name = "%s%d" % (which, u)
-            ww[(which, u)] = const.tile([P, 512], U32, name="ww" + name, tag="ww" + name, align_bytes=64)
-            ws[(which, u)] = const.tile([P, 512], U8, name="ws" + name, tag="ws" + name, align_bytes=64)
-            pending.append(lambda: quantise(grp, 512, ww[(which, u)], ws[(which, u)]))
-
-        def prep_h0(g):
-            grp = new_grp()
-            g32 = grp[:].bitcast(F32)
-            banks = []
-            for b2 in range(CHUNK_TILES[0] // 2):
-                bank = pro_bank()
-                transpose_pairs(bank, h32[0], [2 * b2, 2 * b2 + 1], 512, g * 256)
-                banks.append(bank)
-            for b2, bank in enumerate(banks):
-                copy_out("act" if b2 % 2 == 0 else "dve", bank, g32[:, b2 * 512 : (b2 + 1) * 512])
-            flush()
-            pending.append(lambda: q_h(0, g, grp))
-
-        prep_w("ls", 0)
-        prep_w("mu", 0)
-        prep_h0(0)
-        prep_h0(1)
-        prep_w("ls", 1)
-        prep_w("mu", 1)
-
-        win_grp = new_grp()
-        win_bank = pro_bank()
-        transpose_pairs(win_bank, win_raw[:].bitcast(F32), [0, 1], 256, 0)
-        copy_out("act", win_bank, win_grp[:].bitcast(F32)[:, 0:512])
-        flush()
-        winw = const.tile([P, HD], U32, name="winw", tag="winw", align_bytes=64)
-        wins = const.tile([P, HD], U8, name="wins", tag="wins", align_bytes=64)
-        quantise(win_grp, HD, winw, wins)
-
-        bin_bank = pro_bank()
-        nc.tensor.matmul(out=bin_bank[:, :HD], lhsT=ones[:], rhs=bin_row[:], start=True, stop=True)
-        bin_bc = const.tile([P, 2 * HD], F32, name="bin_bc", tag="bin_bc")
-        nc.vector.tensor_copy(out=bin_bc[:, :HD], in_=bin_bank[:, :HD])
-        nc.vector.tensor_copy(out=bin_bc[:, HD:], in_=bin_bank[:, :HD])
-
-        zp = {}
-        zw = {}
-        zs = {}
+        def tr_e(c, u):
+            e_bank = ps_e.tile([P, 512], F32, name="e_bank", tag="e_bank")
+            for i in range(CHUNK_TILES[c]):
+                w0 = i * 256 + u * P
+                nc.tensor.transpose(
+                    out=e_bank[:, i * P : (i + 1) * P], in_=e32[c][:, w0 : w0 + P], identity=ident[:]
+                )
+            return e_bank
 
         def mx1(which, c, u, e):
             n = width[c]
-            acc = ps_mm.tile([P, 512], F32, name="acc", tag="acc")
+            acc = bank_of("mm")
             for g in range(2):
                 col = g * 256 + e * P
                 nc.tensor.matmul_mx(
@@ -243,6 +221,35 @@ def tile_vae_pa_t_kernel(
                     stop=(g == 1),
                 )
             return acc
+
+        def do_exp(c, u, ls):
+            n = width[c]
+            s_t = []
+            for e in range(2):
+                t = 2 * u + e
+                s = spool.tile([P, 512], F32, name="s", tag="s")
+                nc.scalar.activation(
+                    out=s[:, :n], in_=ls[e][:, :n], func=AF.Exp, bias=blsh[:, t : t + 1], scale=0.5
+                )
+                s_t.append(s)
+            return s_t
+
+        def do_a(c, u, e_bank, s_t):
+            n = width[c]
+            e_view = e_bank[:, :n].bitcast(BF16).rearrange("p (n e) -> p e n", e=2)
+            tts = []
+            for e in range(2):
+                tt = spool.tile([P, 512], F32, name="tt", tag="tt")
+                nc.vector.tensor_tensor(
+                    out=tt[:, :n], in0=e_view[:, e, :], in1=s_t[e][:, :n], op=ALU.mult
+                )
+                tts.append(tt)
+            return tts
+
+        zp = {}
+        zg = {}
+        zw = {}
+        zs = {}
 
         def do_b(c, u, mu, tt):
             n = width[c]
@@ -258,8 +265,6 @@ def tile_vae_pa_t_kernel(
                     op0=ALU.add,
                     op1=ALU.add,
                 )
-
-        zg = {}
 
         def regroup(c, engine):
             n = width[c]
@@ -284,8 +289,8 @@ def tile_vae_pa_t_kernel(
             zs[c] = zwpool.tile([P, 512], U8, name="zs", tag="zs", align_bytes=64)
             quantise(zg[c], width[c], zw[c], zs[c])
 
-        def do_s(c, unit, pool, name):
-            o = pool.tile([P, 512], F32, name=name, tag=name)
+        def do_s(c, unit, pool):
+            o = bank_of(pool)
             for j in range(2):
                 i = 2 * unit + j
                 nc.tensor.matmul_mx(
@@ -305,6 +310,13 @@ def tile_vae_pa_t_kernel(
             nc.vector.tensor_tensor(out=o_sb[:], in0=o[:], in1=bin_bc[:], op=ALU.add)
             return (c, unit, o_sb)
 
+        def do_add_pool(item):
+            c, unit, o = item
+            o_sb = opool.tile([P, 512], F32, name="o_sb", tag="o_sb")
+            nc.scalar.copy(out=o_sb[:], in_=o[:])
+            nc.gpsimd.tensor_tensor(out=o_sb[:], in0=o_sb[:], in1=bin_bc[:], op=ALU.add)
+            return (c, unit, o_sb)
+
         def do_tanh_store(item):
             c, unit, o_sb = item
             nc.scalar.activation(out=o_sb[:], in_=o_sb[:], func=AF.Tanh)
@@ -313,76 +325,105 @@ def tile_vae_pa_t_kernel(
             )
             nc.sync.dma_start(out=view[:, unit * 512 : (unit + 1) * 512], in_=o_sb[:])
 
-        pend_b = None
+        bin_bank = bank_of("o")
+        nc.tensor.matmul(out=bin_bank[:, :HD], lhsT=ones[:], rhs=bin_row[:], start=True, stop=True)
+        bin_bc = const.tile([P, 2 * HD], F32, name="bin_bc", tag="bin_bc")
+        nc.vector.tensor_copy(out=bin_bc[:, :HD], in_=bin_bank[:, :HD])
+        nc.vector.tensor_copy(out=bin_bc[:, HD:], in_=bin_bank[:, :HD])
+        bmu = const.tile([P, 4], F32, name="bmu", tag="bmu")
+        blsh = const.tile([P, 4], F32, name="blsh", tag="blsh")
+        nc.vector.tensor_copy(out=bmu[:], in_=bmu_raw[:])
+        nc.vector.tensor_scalar_mul(out=blsh[:], in0=bls_raw[:], scalar1=0.5)
+
+        g_ls0 = copy_banks(tr_w("ls", 0, "mm"), ["act", "dve"])
+        g_h00 = copy_banks(tr_h(0, 0, "xy"), ["act", "dve"])
+        q_w("ls", 0, g_ls0)
+        g_h01 = copy_banks(tr_h(0, 1, "mm"), ["act", "dve"])
+        q_h(0, 0, g_h00)
+        g_mu0 = copy_banks(tr_w("mu", 0, "xy"), ["act"])
+        q_h(0, 1, g_h01)
+        q_w("mu", 0, g_mu0)
+        g_ls1 = copy_banks(tr_w("ls", 1, "mm"), ["act", "dve"])
+        q_w("ls", 1, g_ls1)
+
+        ls = [mx1("ls", 0, 0, e) for e in range(2)]
+        mu = [mx1("mu", 0, 0, e) for e in range(2)]
+        s_t = do_exp(0, 0, ls)
+        g_mu1 = copy_banks(tr_w("mu", 1, "xy"), ["act", "dve"])
+        e_bank = tr_e(0, 0)
+        q_w("mu", 1, g_mu1)
+        tts = do_a(0, 0, e_bank, s_t)
+        ls = [mx1("ls", 0, 1, e) for e in range(2)]
+        do_b(0, 0, mu, tts)
+        s_t = do_exp(0, 1, ls)
+
+        banks10 = tr_h(1, 0, "xy")
+        e_bank = tr_e(0, 1)
+        win_bank = bank_of("o")
+        transpose_pairs(win_bank, win_raw[:].bitcast(F32), [0, 1], 256, 0)
+        g_h10 = copy_banks(banks10, ["act", "dve"])
+        banks11 = tr_h(1, 1, "xy")
+        g_win = copy_banks([win_bank], ["act"])
+        q_h(1, 0, g_h10)
+        tts = do_a(0, 1, e_bank, s_t)
+        mu = [mx1("mu", 0, 1, e) for e in range(2)]
+        g_h11 = copy_banks(banks11, ["act", "dve"])
+        winw = const.tile([P, HD], U32, name="winw", tag="winw", align_bytes=64)
+        wins = const.tile([P, HD], U8, name="wins", tag="wins", align_bytes=64)
+        quantise(g_win, HD, winw, wins)
+        q_h(1, 1, g_h11)
+        pend_b = (0, 1, mu, tts)
+
         pend_add = []
+        added_late = []
         s_fifo = []
         s_head = 0
-        for c in range(n_chunks):
-            n = width[c]
-            nb = CHUNK_TILES[c]
+        for c in range(1, n_chunks):
+            nxt = c + 1 < n_chunks
+            grp = [None, None]
             for u in range(2):
-                nxt = c + 1 < n_chunks
-                banks = []
+                banks = tr_h(c + 1, u, "xy") if nxt else []
+                e_bank = tr_e(c, u)
+                do_b(*pend_b)
                 if nxt:
-                    for b2 in range(CHUNK_TILES[c + 1] // 2):
-                        bank = ps_xy.tile([P, 512], F32, name="xy", tag="xy")
-                        transpose_pairs(bank, h32[c + 1], [2 * b2, 2 * b2 + 1], 512, u * 256)
-                        banks.append(bank)
-                e_bank = ps_e.tile([P, 512], F32, name="e_bank", tag="e_bank")
-                for i in range(nb):
-                    w0 = i * 256 + u * P
-                    nc.tensor.transpose(
-                        out=e_bank[:, i * P : (i + 1) * P], in_=e32[c][:, w0 : w0 + P], identity=ident[:]
-                    )
-                if pend_b is not None:
-                    do_b(*pend_b)
-                grp = None
-                if nxt:
-                    grp = new_grp()
-                    g32 = grp[:].bitcast(F32)
-                    for b2, bank in enumerate(banks):
-                        copy_out("act", bank, g32[:, b2 * 512 : (b2 + 1) * 512])
-                if u == 0 and c >= 1:
+                    grp[u] = copy_banks(banks, ["act"])
+                if u == 0:
                     regroup(c - 1, REGROUP)
-                added = [do_add(item) for item in pend_add]
+                added = added_late + [do_add(item) for item in pend_add]
                 pend_add = []
-                if u == 1 and c >= 1:
+                added_late = []
+                if u == 1:
                     q_z(c - 1)
                     s_fifo.extend([(c - 1, unit) for unit in range(CHUNK_TILES[c - 1] // 2)])
-                if nxt:
-                    q_h(c + 1, u, grp)
+                    if nxt:
+                        q_h(c + 1, 0, grp[0])
                 ls = [mx1("ls", c, u, e) for e in range(2)]
-                if s_head < len(s_fifo):
-                    sc, su = s_fifo[s_head]
-                    s_head += 1
-                    pend_add.append(do_s(sc, su, ps_o, "o_bank"))
                 mu = [mx1("mu", c, u, e) for e in range(2)]
-                s_t = []
-                for e in range(2):
-                    t = 2 * u + e
-                    s = spool.tile([P, 512], F32, name="s", tag="s")
-                    nc.scalar.activation(
-                        out=s[:, :n], in_=ls[e][:, :n], func=AF.Exp, bias=blsh[:, t : t + 1], scale=0.5
-                    )
-                    s_t.append(s)
+                o_item = None
+                if s_head < len(s_fifo):
+                    o_item = do_s(s_fifo[s_head][0], s_fifo[s_head][1], "o")
+                    s_head += 1
+                s_t = do_exp(c, u, ls)
+                if o_item is not None:
+                    if POOL_ADD_EVERY > 0 and s_head % POOL_ADD_EVERY == 0:
+                        added_late.append(do_add_pool(o_item))
+                    else:
+                        pend_add.append(o_item)
                 for item in added:
                     do_tanh_store(item)
-                e_view = e_bank[:, :n].bitcast(BF16).rearrange("p (n e) -> p e n", e=2)
-                tts = []
-                for e in range(2):
-                    tt = spool.tile([P, 512], F32, name="tt", tag="tt")
-                    nc.vector.tensor_tensor(out=tt[:, :n], in0=e_view[:, e, :], in1=s_t[e][:, :n], op=ALU.mult)
-                    tts.append(tt)
+                tts = do_a(c, u, e_bank, s_t)
+                if u == 1 and nxt:
+                    q_h(c + 1, 1, grp[1])
                 pend_b = (c, u, mu, tts)
 
         last = n_chunks - 1
         do_b(*pend_b)
         for sc, su in s_fifo[s_head:]:
-            pend_add.append(do_s(sc, su, ps_mm, "acc"))
+            pend_add.append(do_s(sc, su, "mm"))
         regroup(last, "dve")
-        added = [do_add(item) for item in pend_add]
+        q_z(last)
+        added = added_late + [do_add(item) for item in pend_add]
         for item in added:
             do_tanh_store(item)
-        q_z(last)
         for unit in range(CHUNK_TILES[last] // 2):
-            do_tanh_store(do_add(do_s(last, unit, ps_mm, "acc")))
+            do_tanh_store(do_add(do_s(last, unit, "mm")))

@@ -15,7 +15,7 @@ P = 128
 B, HE, Z, HD = 4096, 1024, 512, 256
 FLOPS = 2 * B * HE * 2 * Z + 2 * B * Z * HD
 
-CHUNK_TILES = [4, 4, 4, 4, 4, 4, 4, 2, 2]
+CHUNK_TILES = [4, 4, 4, 4, 4, 4, 4, 4]
 MANUAL = True
 REGROUP = "pool"
 POOL_ADD_EVERY = 0
@@ -325,52 +325,43 @@ def tile_vae_pa_t_kernel(
             )
             nc.sync.dma_start(out=view[:, unit * 512 : (unit + 1) * 512], in_=o_sb[:])
 
-        bin_bank = bank_of("o")
-        nc.tensor.matmul(out=bin_bank[:, :HD], lhsT=ones[:], rhs=bin_row[:], start=True, stop=True)
-        bin_bc = const.tile([P, 2 * HD], F32, name="bin_bc", tag="bin_bc")
-        nc.vector.tensor_copy(out=bin_bc[:, :HD], in_=bin_bank[:, :HD])
-        nc.vector.tensor_copy(out=bin_bc[:, HD:], in_=bin_bank[:, :HD])
         bmu = const.tile([P, 4], F32, name="bmu", tag="bmu")
         blsh = const.tile([P, 4], F32, name="blsh", tag="blsh")
-        nc.vector.tensor_copy(out=bmu[:], in_=bmu_raw[:])
-        nc.vector.tensor_scalar_mul(out=blsh[:], in0=bls_raw[:], scalar1=0.5)
+        bin_bc = const.tile([P, 2 * HD], F32, name="bin_bc", tag="bin_bc")
+        winw = const.tile([P, HD], U32, name="winw", tag="winw", align_bytes=64)
+        wins = const.tile([P, HD], U8, name="wins", tag="wins", align_bytes=64)
 
-        g_ls0 = copy_banks(tr_w("ls", 0, "mm"), ["act", "dve"])
+        g_ls0 = copy_banks(tr_w("ls", 0, "mm"), ["act"])
         g_h00 = copy_banks(tr_h(0, 0, "xy"), ["act", "dve"])
         q_w("ls", 0, g_ls0)
         g_h01 = copy_banks(tr_h(0, 1, "mm"), ["act", "dve"])
         q_h(0, 0, g_h00)
         g_mu0 = copy_banks(tr_w("mu", 0, "xy"), ["act"])
         q_h(0, 1, g_h01)
+        nc.vector.tensor_copy(out=bmu[:], in_=bmu_raw[:])
+        nc.vector.tensor_scalar_mul(out=blsh[:], in0=bls_raw[:], scalar1=0.5)
+        g_ls1 = copy_banks(tr_w("ls", 1, "mm"), ["act"])
         q_w("mu", 0, g_mu0)
-        g_ls1 = copy_banks(tr_w("ls", 1, "mm"), ["act", "dve"])
-        q_w("ls", 1, g_ls1)
-
+        banks_mu1 = tr_w("mu", 1, "xy")
         ls = [mx1("ls", 0, 0, e) for e in range(2)]
-        mu = [mx1("mu", 0, 0, e) for e in range(2)]
         s_t = do_exp(0, 0, ls)
-        g_mu1 = copy_banks(tr_w("mu", 1, "xy"), ["act", "dve"])
+        g_mu1 = copy_banks(banks_mu1, ["act"])
+        q_w("ls", 1, g_ls1)
         e_bank = tr_e(0, 0)
-        q_w("mu", 1, g_mu1)
+        mu = [mx1("mu", 0, 0, e) for e in range(2)]
         tts = do_a(0, 0, e_bank, s_t)
+        banks10 = tr_h(1, 0, "xy")
         ls = [mx1("ls", 0, 1, e) for e in range(2)]
+        q_w("mu", 1, g_mu1)
+        g_h10 = copy_banks(banks10, ["act"])
         do_b(0, 0, mu, tts)
         s_t = do_exp(0, 1, ls)
-
-        banks10 = tr_h(1, 0, "xy")
         e_bank = tr_e(0, 1)
-        win_bank = bank_of("o")
-        transpose_pairs(win_bank, win_raw[:].bitcast(F32), [0, 1], 256, 0)
-        g_h10 = copy_banks(banks10, ["act", "dve"])
         banks11 = tr_h(1, 1, "xy")
-        g_win = copy_banks([win_bank], ["act"])
+        mu = [mx1("mu", 0, 1, e) for e in range(2)]
+        g_h11 = copy_banks(banks11, ["act"])
         q_h(1, 0, g_h10)
         tts = do_a(0, 1, e_bank, s_t)
-        mu = [mx1("mu", 0, 1, e) for e in range(2)]
-        g_h11 = copy_banks(banks11, ["act", "dve"])
-        winw = const.tile([P, HD], U32, name="winw", tag="winw", align_bytes=64)
-        wins = const.tile([P, HD], U8, name="wins", tag="wins", align_bytes=64)
-        quantise(g_win, HD, winw, wins)
         q_h(1, 1, g_h11)
         pend_b = (0, 1, mu, tts)
 
@@ -384,26 +375,42 @@ def tile_vae_pa_t_kernel(
             for u in range(2):
                 banks = tr_h(c + 1, u, "xy") if nxt else []
                 e_bank = tr_e(c, u)
+                first = c == 1 and u == 0
+                if first:
+                    win_bank = bank_of("o")
+                    transpose_pairs(win_bank, win_raw[:].bitcast(F32), [0, 1], 256, 0)
                 do_b(*pend_b)
                 if nxt:
                     grp[u] = copy_banks(banks, ["act"])
+                if first:
+                    g_win = copy_banks([win_bank], ["act"])
                 if u == 0:
                     regroup(c - 1, REGROUP)
                 added = added_late + [do_add(item) for item in pend_add]
                 pend_add = []
                 added_late = []
                 if u == 1:
+                    if c == 1:
+                        quantise(g_win, HD, winw, wins)
                     q_z(c - 1)
                     s_fifo.extend([(c - 1, unit) for unit in range(CHUNK_TILES[c - 1] // 2)])
                     if nxt:
                         q_h(c + 1, 0, grp[0])
                 ls = [mx1("ls", c, u, e) for e in range(2)]
                 mu = [mx1("mu", c, u, e) for e in range(2)]
+                if first:
+                    bin_bank = bank_of("o")
+                    nc.tensor.matmul(
+                        out=bin_bank[:, :HD], lhsT=ones[:], rhs=bin_row[:], start=True, stop=True
+                    )
                 o_item = None
                 if s_head < len(s_fifo):
                     o_item = do_s(s_fifo[s_head][0], s_fifo[s_head][1], "o")
                     s_head += 1
                 s_t = do_exp(c, u, ls)
+                if first:
+                    nc.scalar.copy(out=bin_bc[:, :HD], in_=bin_bank[:, :HD])
+                    nc.scalar.copy(out=bin_bc[:, HD:], in_=bin_bank[:, :HD])
                 if o_item is not None:
                     if POOL_ADD_EVERY > 0 and s_head % POOL_ADD_EVERY == 0:
                         added_late.append(do_add_pool(o_item))
@@ -425,5 +432,6 @@ def tile_vae_pa_t_kernel(
         added = added_late + [do_add(item) for item in pend_add]
         for item in added:
             do_tanh_store(item)
-        for unit in range(CHUNK_TILES[last] // 2):
-            do_tanh_store(do_add(do_s(last, unit, "mm")))
+        items = [do_s(last, unit, "mm") for unit in range(CHUNK_TILES[last] // 2)]
+        for item in items:
+            do_tanh_store(do_add(item))

@@ -16,7 +16,7 @@ B, HE, Z, HD = 4096, 1024, 512, 256
 FLOPS = 2 * B * HE * 2 * Z + 2 * B * Z * HD
 
 CHUNK_TILES = [4, 4, 4, 4, 4, 4, 4, 4]
-MANUAL = True
+MANUAL = False
 REGROUP = "pool"
 POOL_ADD_EVERY = 0
 

@@ -16,7 +16,7 @@ B, HE, Z, HD = 4096, 1024, 512, 256
 FLOPS = 2 * B * HE * 2 * Z + 2 * B * Z * HD
 
 CHUNK_TILES = [4, 4, 4, 4, 4, 4, 4, 4]
-MANUAL = False
+MANUAL = True
 REGROUP = "pool"
 POOL_ADD_EVERY = 0
 
@@ -381,7 +381,7 @@ def tile_vae_pa_t_kernel(
                     transpose_pairs(win_bank, win_raw[:].bitcast(F32), [0, 1], 256, 0)
                 do_b(*pend_b)
                 if nxt:
-                    grp[u] = copy_banks(banks, ["act"])
+                    grp[u] = copy_banks(banks, ["act", "dve"])
                 if first:
                     g_win = copy_banks([win_bank], ["act"])
                 if u == 0:

from contextlib import ExitStack

import concourse.mybir as mybir
from concourse.masks import make_identity

F32 = mybir.dt.float32
BF16 = mybir.dt.bfloat16
U32 = mybir.dt.uint32
U8 = mybir.dt.uint8
FP8X4 = mybir.dt.float8_e4m3fn_x4
AF = mybir.ActivationFunctionType
ALU = mybir.AluOpType

P = 128
B, HE, Z, HD = 4096, 1024, 512, 256
FLOPS = 2 * B * HE * 2 * Z + 2 * B * Z * HD

CHUNK_TILES = [4, 4, 4, 4, 4, 4, 4, 4]
MANUAL = True
REGROUP = "pool"
POOL_ADD_EVERY = 0


def tile_vae_pa_t_kernel(
    tc, h, W_mu_e, b_mu_e, W_ls_e, b_ls_e, eps_z, W_in_d, b_in_d, out
):
    nc = tc.nc
    n_chunks = len(CHUNK_TILES)
    row0 = [P * sum(CHUNK_TILES[:c]) for c in range(n_chunks)]
    width = [P * nb for nb in CHUNK_TILES]

    with ExitStack() as ctx:
        const = ctx.enter_context(tc.tile_pool(name="const", bufs=1))
        gpool = ctx.enter_context(tc.tile_pool(name="gpool", bufs=4))
        wpool = ctx.enter_context(tc.tile_pool(name="wpool", bufs=6))
        spool = ctx.enter_context(tc.tile_pool(name="spool", bufs=4))
        zpool = ctx.enter_context(tc.tile_pool(name="zpool", bufs=2))
        zwpool = ctx.enter_context(tc.tile_pool(name="zwpool", bufs=3))
        opool = ctx.enter_context(tc.tile_pool(name="opool", bufs=8))
        ps_xy = ctx.enter_context(tc.psum_pool(name="ps_xy", bufs=2))
        ps_e = ctx.enter_context(tc.psum_pool(name="ps_e", bufs=1))
        ps_o = ctx.enter_context(tc.psum_pool(name="ps_o", bufs=1))
        ps_mm = ctx.enter_context(tc.psum_pool(name="ps_mm", bufs=4))
        if MANUAL:
            ctx.enter_context(tc.manual_schedule())

        w_src = {"ls": W_ls_e, "mu": W_mu_e}
        w_raw = {}
        for u in range(2):
            for which in ("ls", "mu"):
                nm = "wraw_%s%d" % (which, u)
                w_raw[(which, u)] = const.tile([P, 2 * HE], BF16, name=nm, tag=nm)
        win_raw = const.tile([P, 2 * Z], BF16, name="win_raw", tag="win_raw")
        h_sb = [
            const.tile([P, CHUNK_TILES[c] * HE], BF16, name="h_sb%d" % c, tag="h_sb%d" % c)
            for c in range(n_chunks)
        ]
        e_sb = [
            const.tile([P, CHUNK_TILES[c] * Z], BF16, name="e_sb%d" % c, tag="e_sb%d" % c)
            for c in range(n_chunks)
        ]

        def load_w(which, u):
            nc.sync.dma_start(
                out=w_raw[(which, u)][:],
                in_=w_src[which][256 * u : 256 * (u + 1), :].rearrange("(p e) k -> p (e k)", e=2),
            )

        def load_h(c):
            nc.sync.dma_start(
                out=h_sb[c][:],
                in_=h[row0[c] : row0[c] + width[c], :].rearrange(
                    "(p i) k -> p (i k)", i=CHUNK_TILES[c]
                ),
            )

        def load_e(c):
            nc.sync.dma_start(
                out=e_sb[c][:],
                in_=eps_z[row0[c] : row0[c] + width[c], :].rearrange(
                    "(p i) k -> p (i k)", i=CHUNK_TILES[c]
                ),
            )

        bmu_raw = const.tile([P, 4], BF16, name="bmu_raw", tag="bmu_raw")
        bls_raw = const.tile([P, 4], BF16, name="bls_raw", tag="bls_raw")
        bin_row = const.tile([P, HD], BF16, name="bin_row", tag="bin_row")
        ones = const.tile([P, P], BF16, name="ones", tag="ones")
        warm = const.tile([P, 1], F32, name="warm", tag="warm")
        warm2 = const.tile([P, 1], F32, name="warm2", tag="warm2")
        nc.vector.memset(warm[:], 0.0)
        nc.vector.memset(bin_row[:], 0.0)
        nc.vector.memset(ones[:], 1.0)
        nc.scalar.dma_start(out=bin_row[0:1, :], in_=b_in_d.rearrange("(o n) -> o n", o=1))
        nc.scalar.dma_start(
            out=bls_raw[:].rearrange("p (u e) -> p u e", u=2),
            in_=b_ls_e.rearrange("(u p e) -> p u e", u=2, e=2),
        )
        nc.scalar.dma_start(
            out=bmu_raw[:].rearrange("p (u e) -> p u e", u=2),
            in_=b_mu_e.rearrange("(u p e) -> p u e", u=2, e=2),
        )
        nc.scalar.activation(out=warm2[:], in_=warm[:], func=AF.Exp)

        load_w("ls", 0)
        load_h(0)
        load_w("mu", 0)
        load_w("ls", 1)
        load_w("mu", 1)
        load_e(0)
        load_h(1)
        load_e(1)
        nc.sync.dma_start(
            out=win_raw[:].rearrange("p (j k) -> p j k", j=2),
            in_=W_in_d.rearrange("(j p) k -> p j k", j=2),
        )
        for c in range(2, n_chunks):
            load_h(c)
            load_e(c)

        ident = const.tile([P, P], F32, name="ident", tag="ident")
        make_identity(nc, ident[:])

        def transpose_pairs(bank, src32, groups, stride, off):
            view = bank[:].rearrange("p (v n) -> p v n", v=2)
            for j, i in enumerate(groups):
                for v in range(2):
                    w0 = i * stride + off + v * P
                    nc.tensor.transpose(
                        out=view[:, v, j * P : (j + 1) * P],
                        in_=src32[:, w0 : w0 + P],
                        identity=ident[:],
                    )

        def copy_out(engine, bank, dst32):
            src = bank[:].rearrange("p (v n) -> p n v", v=2)
            dst = dst32.rearrange("p (n v) -> p n v", v=2)
            if engine == "act":
                nc.scalar.copy(out=dst, in_=src)
            else:
                nc.vector.tensor_copy(out=dst, in_=src)

        def quantise(grp, cols, words, scales):
            nc.vector.quantize_mx(
                out=words[:, :cols].bitcast(FP8X4), scales=scales[:, :cols], in_=grp[:, : 4 * cols]
            )

        def bank_of(pool):
            if pool == "xy":
                return ps_xy.tile([P, 512], F32, name="xy", tag="xy")
            if pool == "o":
                return ps_o.tile([P, 512], F32, name="o_bank", tag="o_bank")
            return ps_mm.tile([P, 512], F32, name="acc", tag="acc")

        def new_grp():
            return gpool.tile([P, 2048], BF16, name="grp", tag="grp", align_bytes=64)

        h32 = [t[:].bitcast(F32) for t in h_sb]
        e32 = [t[:].bitcast(F32) for t in e_sb]
        hw = {}
        hs = {}
        ww = {}
        ws = {}

        def tr_w(which, u, pool):
            raw32 = w_raw[(which, u)][:].bitcast(F32)
            banks = []
            for g in range(2):
                bank = bank_of(pool)
                transpose_pairs(bank, raw32, [0, 1], 512, g * 256)
                banks.append(bank)
            return banks

        def tr_h(c, g, pool):
            banks = []
            for b2 in range(CHUNK_TILES[c] // 2):
                bank = bank_of(pool)
                transpose_pairs(bank, h32[c], [2 * b2, 2 * b2 + 1], 512, g * 256)
                banks.append(bank)
            return banks

        def copy_banks(banks, engines):
            grp = new_grp()
            g32 = grp[:].bitcast(F32)
            for k, bank in enumerate(banks):
                copy_out(engines[k % len(engines)], bank, g32[:, k * 512 : (k + 1) * 512])
            return grp

        def q_w(which, u, grp):
            nm = "%s%d" % (which, u)
            ww[(which, u)] = const.tile([P, 512], U32, name="ww" + nm, tag="ww" + nm, align_bytes=64)
            ws[(which, u)] = const.tile([P, 512], U8, name="ws" + nm, tag="ws" + nm, align_bytes=64)
            quantise(grp, 512, ww[(which, u)], ws[(which, u)])

        def q_h(c, g, grp):
            hw[(c, g)] = wpool.tile([P, 512], U32, name="hw", tag="hw", align_bytes=64)
            hs[(c, g)] = wpool.tile([P, 512], U8, name="hs", tag="hs", align_bytes=64)
            quantise(grp, width[c], hw[(c, g)], hs[(c, g)])

        def tr_e(c, u):
            e_bank = ps_e.tile([P, 512], F32, name="e_bank", tag="e_bank")
            for i in range(CHUNK_TILES[c]):
                w0 = i * 256 + u * P
                nc.tensor.transpose(
                    out=e_bank[:, i * P : (i + 1) * P], in_=e32[c][:, w0 : w0 + P], identity=ident[:]
                )
            return e_bank

        def mx1(which, c, u, e):
            n = width[c]
            acc = bank_of("mm")
            for g in range(2):
                col = g * 256 + e * P
                nc.tensor.matmul_mx(
                    out=acc[:, :n],
                    lhsT=ww[(which, u)][:, col : col + P].bitcast(FP8X4),
                    lhsT_scale=ws[(which, u)][:, col : col + P],
                    rhs=hw[(c, g)][:, :n].bitcast(FP8X4),
                    rhs_scale=hs[(c, g)][:, :n],
                    start=(g == 0),
                    stop=(g == 1),
                )
            return acc

        def do_exp(c, u, ls):
            n = width[c]
            s_t = []
            for e in range(2):
                t = 2 * u + e
                s = spool.tile([P, 512], F32, name="s", tag="s")
                nc.scalar.activation(
                    out=s[:, :n], in_=ls[e][:, :n], func=AF.Exp, bias=blsh[:, t : t + 1], scale=0.5
                )
                s_t.append(s)
            return s_t

        def do_a(c, u, e_bank, s_t):
            n = width[c]
            e_view = e_bank[:, :n].bitcast(BF16).rearrange("p (n e) -> p e n", e=2)
            tts = []
            for e in range(2):
                tt = spool.tile([P, 512], F32, name="tt", tag="tt")
                nc.vector.tensor_tensor(
                    out=tt[:, :n], in0=e_view[:, e, :], in1=s_t[e][:, :n], op=ALU.mult
                )
                tts.append(tt)
            return tts

        zp = {}
        zg = {}
        zw = {}
        zs = {}

        def do_b(c, u, mu, tt):
            n = width[c]
            if u == 0:
                zp[c] = zpool.tile([P, 4, 512], BF16, name="zp", tag="zp")
            for e in range(2):
                t = 2 * u + e
                nc.vector.scalar_tensor_tensor(
                    out=zp[c][:, t, :n],
                    in0=mu[e][:, :n],
                    scalar=bmu[:, t : t + 1],
                    in1=tt[e][:, :n],
                    op0=ALU.add,
                    op1=ALU.add,
                )

        def regroup(c, engine):
            n = width[c]
            zg[c] = zpool.tile([P, 2048], BF16, name="zg", tag="zg", align_bytes=64)
            if engine == "pool":
                nc.gpsimd.tensor_scalar(
                    out=zg[c][:, : 4 * n].rearrange("p (n t) -> p n t", t=4),
                    in0=zp[c][:, :, :n].rearrange("p t n -> p n t"),
                    scalar1=1.0,
                    scalar2=0.0,
                    op0=ALU.mult,
                    op1=ALU.add,
                )
            else:
                nc.vector.tensor_copy(
                    out=zg[c][:, : 4 * n].rearrange("p (c i t) -> p c t i", i=4, t=4),
                    in_=zp[c][:, :, :n].rearrange("p t (c i) -> p c t i", i=4),
                )

        def q_z(c):
            zw[c] = zwpool.tile([P, 512], U32, name="zw", tag="zw", align_bytes=64)
            zs[c] = zwpool.tile([P, 512], U8, name="zs", tag="zs", align_bytes=64)
            quantise(zg[c], width[c], zw[c], zs[c])

        def do_s(c, unit, pool):
            o = bank_of(pool)
            for j in range(2):
                i = 2 * unit + j
                nc.tensor.matmul_mx(
                    out=o[:, j * HD : (j + 1) * HD],
                    lhsT=zw[c][:, i * P : (i + 1) * P].bitcast(FP8X4),
                    lhsT_scale=zs[c][:, i * P : (i + 1) * P],
                    rhs=winw[:].bitcast(FP8X4),
                    rhs_scale=wins[:],
                    start=True,
                    stop=True,
                )
            return (c, unit, o)

        def do_add(item):
            c, unit, o = item
            o_sb = opool.tile([P, 512], F32, name="o_sb", tag="o_sb")
            nc.vector.tensor_tensor(out=o_sb[:], in0=o[:], in1=bin_bc[:], op=ALU.add)
            return (c, unit, o_sb)

        def do_add_pool(item):
            c, unit, o = item
            o_sb = opool.tile([P, 512], F32, name="o_sb", tag="o_sb")
            nc.scalar.copy(out=o_sb[:], in_=o[:])
            nc.gpsimd.tensor_tensor(out=o_sb[:], in0=o_sb[:], in1=bin_bc[:], op=ALU.add)
            return (c, unit, o_sb)

        def do_tanh_store(item):
            c, unit, o_sb = item
            nc.scalar.activation(out=o_sb[:], in_=o_sb[:], func=AF.Tanh)
            view = out[row0[c] : row0[c] + width[c], :].rearrange(
                "(p i) d -> p (i d)", i=CHUNK_TILES[c]
            )
            nc.sync.dma_start(out=view[:, unit * 512 : (unit + 1) * 512], in_=o_sb[:])

        bmu = const.tile([P, 4], F32, name="bmu", tag="bmu")
        blsh = const.tile([P, 4], F32, name="blsh", tag="blsh")
        bin_bc = const.tile([P, 2 * HD], F32, name="bin_bc", tag="bin_bc")
        winw = const.tile([P, HD], U32, name="winw", tag="winw", align_bytes=64)
        wins = const.tile([P, HD], U8, name="wins", tag="wins", align_bytes=64)

        g_ls0 = copy_banks(tr_w("ls", 0, "mm"), ["act"])
        g_h00 = copy_banks(tr_h(0, 0, "xy"), ["act", "dve"])
        q_w("ls", 0, g_ls0)
        g_h01 = copy_banks(tr_h(0, 1, "mm"), ["act", "dve"])
        q_h(0, 0, g_h00)
        g_mu0 = copy_banks(tr_w("mu", 0, "xy"), ["act"])
        q_h(0, 1, g_h01)
        nc.vector.tensor_copy(out=bmu[:], in_=bmu_raw[:])
        nc.vector.tensor_scalar_mul(out=blsh[:], in0=bls_raw[:], scalar1=0.5)
        g_ls1 = copy_banks(tr_w("ls", 1, "mm"), ["act"])
        q_w("mu", 0, g_mu0)
        banks_mu1 = tr_w("mu", 1, "xy")
        ls = [mx1("ls", 0, 0, e) for e in range(2)]
        s_t = do_exp(0, 0, ls)
        g_mu1 = copy_banks(banks_mu1, ["act"])
        q_w("ls", 1, g_ls1)
        e_bank = tr_e(0, 0)
        mu = [mx1("mu", 0, 0, e) for e in range(2)]
        tts = do_a(0, 0, e_bank, s_t)
        banks10 = tr_h(1, 0, "xy")
        ls = [mx1("ls", 0, 1, e) for e in range(2)]
        q_w("mu", 1, g_mu1)
        g_h10 = copy_banks(banks10, ["act"])
        do_b(0, 0, mu, tts)
        s_t = do_exp(0, 1, ls)
        e_bank = tr_e(0, 1)
        banks11 = tr_h(1, 1, "xy")
        mu = [mx1("mu", 0, 1, e) for e in range(2)]
        g_h11 = copy_banks(banks11, ["act"])
        q_h(1, 0, g_h10)
        tts = do_a(0, 1, e_bank, s_t)
        q_h(1, 1, g_h11)
        pend_b = (0, 1, mu, tts)

        pend_add = []
        added_late = []
        s_fifo = []
        s_head = 0
        for c in range(1, n_chunks):
            nxt = c + 1 < n_chunks
            grp = [None, None]
            for u in range(2):
                banks = tr_h(c + 1, u, "xy") if nxt else []
                e_bank = tr_e(c, u)
                first = c == 1 and u == 0
                if first:
                    win_bank = bank_of("o")
                    transpose_pairs(win_bank, win_raw[:].bitcast(F32), [0, 1], 256, 0)
                do_b(*pend_b)
                if nxt:
                    grp[u] = copy_banks(banks, ["act", "dve"])
                if first:
                    g_win = copy_banks([win_bank], ["act"])
                if u == 0:
                    regroup(c - 1, REGROUP)
                added = added_late + [do_add(item) for item in pend_add]
                pend_add = []
                added_late = []
                if u == 1:
                    if c == 1:
                        quantise(g_win, HD, winw, wins)
                    q_z(c - 1)
                    s_fifo.extend([(c - 1, unit) for unit in range(CHUNK_TILES[c - 1] // 2)])
                    if nxt:
                        q_h(c + 1, 0, grp[0])
                ls = [mx1("ls", c, u, e) for e in range(2)]
                mu = [mx1("mu", c, u, e) for e in range(2)]
                if first:
                    bin_bank = bank_of("o")
                    nc.tensor.matmul(
                        out=bin_bank[:, :HD], lhsT=ones[:], rhs=bin_row[:], start=True, stop=True
                    )
                o_item = None
                if s_head < len(s_fifo):
                    o_item = do_s(s_fifo[s_head][0], s_fifo[s_head][1], "o")
                    s_head += 1
                s_t = do_exp(c, u, ls)
                if first:
                    nc.scalar.copy(out=bin_bc[:, :HD], in_=bin_bank[:, :HD])
                    nc.scalar.copy(out=bin_bc[:, HD:], in_=bin_bank[:, :HD])
                if o_item is not None:
                    if POOL_ADD_EVERY > 0 and s_head % POOL_ADD_EVERY == 0:
                        added_late.append(do_add_pool(o_item))
                    else:
                        pend_add.append(o_item)
                for item in added:
                    do_tanh_store(item)
                tts = do_a(c, u, e_bank, s_t)
                if u == 1 and nxt:
                    q_h(c + 1, 1, grp[1])
                pend_b = (c, u, mu, tts)

        last = n_chunks - 1
        do_b(*pend_b)
        for sc, su in s_fifo[s_head:]:
            pend_add.append(do_s(sc, su, "mm"))
        regroup(last, "dve")
        q_z(last)
        added = added_late + [do_add(item) for item in pend_add]
        for item in added:
            do_tanh_store(item)
        items = [do_s(last, unit, "mm") for unit in range(CHUNK_TILES[last] // 2)]
        for item in items:
            do_tanh_store(do_add(item))
